import numpy as np
import ml_dtypes


BF16 = ml_dtypes.bfloat16


def bf(x):
    return np.asarray(x, np.float32).astype(BF16)


def f64(x):
    return np.asarray(x).astype(np.float64)


E2M1 = np.array([0.0, 0.5, 1.0, 1.5, 2.0, 3.0, 4.0, 6.0, -0.0, -0.5, -1.0, -1.5, -2.0, -3.0, -4.0, -6.0])


def pack_weight(w, fmt):
    k, n = w.shape
    w = f64(bf(w)).reshape(k // 32, 32, n)
    amax = np.abs(w).max(1)
    if fmt == "e4m3":
        byte = np.frexp(amax)[1] - 1 + 127 - 7
    else:
        mant, ex = np.frexp(amax / 6.0)
        byte = np.where(mant > 0.5, ex, ex - 1) + 127
    byte = np.clip(np.where(amax > 0, byte, 1), 1, 254)
    scaled = (w * np.exp2(127.0 - byte)[:, None, :]).reshape(k, n).astype(np.float32)
    by_word = np.ascontiguousarray(scaled.reshape(k // 512, 128, 4, n).transpose(0, 1, 3, 2))
    if fmt == "e4m3":
        words = by_word.astype(ml_dtypes.float8_e4m3fn).view(np.uint8)
    else:
        c = by_word.astype(ml_dtypes.float4_e2m1fn).view(np.uint8) & 0xF
        words = c[..., 0::2] | (c[..., 1::2] << 4)
    return np.ascontiguousarray(words), np.ascontiguousarray(byte.astype(np.uint8).reshape(k // 512, 16, n))


def unpack_weight(words, scales, fmt):
    g, p, n, _ = words.shape
    if fmt == "e4m3":
        vals = np.ascontiguousarray(words).view(ml_dtypes.float8_e4m3fn).astype(np.float64)
    else:
        nib = np.empty((g, p, n, 4), np.uint8)
        nib[..., 0::2] = words & 0xF
        nib[..., 1::2] = words >> 4
        vals = E2M1[nib]
    vals = vals * np.repeat(np.exp2(scales.astype(np.float64) - 127.0), 8, axis=1)[..., None]
    return vals.transpose(0, 1, 3, 2).reshape(g * 512, n)

def pack4(w):
    words, scales = pack_weight(w, "e2m1")
    return words.reshape(words.shape[0], 128, -1), scales


def unpack4(words, scales):
    return unpack_weight(words.reshape(words.shape[0], 128, -1, 2), scales, "e2m1")


def kspread(k):
    return np.exp2(np.repeat(np.random.randint(-6, 7, k // 32), 32).astype(np.float64))


B, S, H, NH, HD = 2, 512, 4096, 16, 128
BASE = 10000.0


def rope_tables():
    inv_freq = 1.0 / BASE ** (np.arange(0, HD, 2) / HD)
    freqs = np.arange(S)[:, None] * inv_freq[None, :]
    emb = np.concatenate([freqs, freqs], axis=-1)
    return np.cos(emb), np.sin(emb)


def rotate_half(u):
    u1, u2 = np.split(u, 2, axis=-1)
    return np.concatenate([-u2, u1], axis=-1)


def setup_inputs():
    s = kspread(H)
    hidden_states = np.random.standard_normal((B, S, H)) * s
    wq = np.random.standard_normal((NH * HD, H)) / np.sqrt(H) / s[None, :]
    wk = np.random.standard_normal((NH * HD, H)) / np.sqrt(H) / s[None, :]
    hidden_states_words, hidden_states_scales = pack4(np.ascontiguousarray(hidden_states.reshape(B * S, H).T))
    wq_words, wq_scales = pack4(np.ascontiguousarray(wq.T))
    wk_words, wk_scales = pack4(np.ascontiguousarray(wk.T))
    return {"hidden_states_words": hidden_states_words, "hidden_states_scales": hidden_states_scales,
            "Wq_words": wq_words, "Wq_scales": wq_scales,
            "Wk_words": wk_words, "Wk_scales": wk_scales}


def reference(hidden_states_words, hidden_states_scales, Wq_words, Wq_scales, Wk_words, Wk_scales):
    xq = unpack4(hidden_states_words, hidden_states_scales).T.reshape(B, S, H)
    q = xq @ unpack4(Wq_words, Wq_scales)
    k = xq @ unpack4(Wk_words, Wk_scales)
    q = q.reshape(B, S, NH, HD).transpose(0, 2, 1, 3)
    k = k.reshape(B, S, NH, HD).transpose(0, 2, 1, 3)
    cos, sin = rope_tables()
    cos = cos[None, None]
    sin = sin[None, None]
    q_rot = q * cos + rotate_half(q) * sin
    k_rot = k * cos + rotate_half(k) * sin
    return q_rot, k_rot

@@ -1,0 +1,214 @@
+import math
+from contextlib import ExitStack
+
+import concourse.mybir as mybir
+
+F32 = mybir.dt.float32
+BF16 = mybir.dt.bfloat16
+I32 = mybir.dt.int32
+U8 = mybir.dt.uint8
+FP4X4 = mybir.dt.float4_e2m1fn_x4
+ACT = mybir.ActivationFunctionType
+ALU = mybir.AluOpType
+
+B, S, H, NH, HD = 2, 512, 4096, 16, 128
+P = 128
+TOKENS = B * S
+FEATURES = NH * HD
+PASSES = H // 512
+COLS = 512
+HEADS = COLS // HD
+HALF = HD // 2
+POS_BLOCKS = S // P
+TOKEN_TILES = TOKENS // P
+W_BLOCKS = 2 * FEATURES // COLS
+BASE = 10000.0
+
+FLOPS = 2 * TOKENS * H * 2 * FEATURES
+
+
+def tile_multiheadattention_pa_kernel(
+    tc, x_words, x_scales, wq_words, wq_scales, wk_words, wk_scales, out_q, out_k
+):
+    nc = tc.nc
+    with ExitStack() as ctx:
+        ctx.enter_context(tc.manual_schedule())
+        keep = ctx.enter_context(tc.tile_pool(name="keep", bufs=1))
+        rope = ctx.enter_context(tc.tile_pool(name="rope", bufs=6))
+        psum = ctx.enter_context(tc.psum_pool(name="psum", bufs=8))
+
+        def new_block(label):
+            codes = keep.tile([P, PASSES, 2 * COLS], U8, name="codes_" + label, align_bytes=256)
+            planes = keep.tile([P, PASSES, COLS], U8, name="planes_" + label, align_bytes=256)
+            return codes, planes
+
+        def zero_planes(engine, block, g0, g1):
+            engine.memset(block[1][:, g0:g1, :].rearrange("p g n -> p (g n)").bitcast(I32), 0)
+
+        def load_codes(block, words, col0, g0, g1):
+            nc.sync.dma_start(
+                out=block[0][:, g0:g1, :],
+                in_=words[g0:g1, :, 2 * col0 : 2 * (col0 + COLS)].rearrange("g p b -> p g b"),
+            )
+
+        def load_scales(block, scales, col0, g0, g1):
+            for q in range(4):
+                nc.sync.dma_start(
+                    out=block[1][32 * q : 32 * q + 4, g0:g1, :].bitcast(I32),
+                    in_=scales[g0:g1, 4 * q : 4 * q + 4, col0 : col0 + COLS]
+                    .rearrange("g r n -> r g n")
+                    .bitcast(I32),
+                )
+
+        x_blocks = [new_block("x%d" % i) for i in range(TOKENS // COLS)]
+        w_blocks = [new_block("w%d" % i) for i in range(W_BLOCKS)]
+
+        def w_source(cb):
+            per = FEATURES // COLS
+            words, scales = (wq_words, wq_scales) if cb < per else (wk_words, wk_scales)
+            return words, scales, (cb % per) * COLS
+
+        def load_w(cb):
+            words, scales, col0 = w_source(cb)
+            load_codes(w_blocks[cb], words, col0, 0, PASSES)
+            load_scales(w_blocks[cb], scales, col0, 0, PASSES)
+
+        warm = keep.tile([P, COLS], BF16, name="warm")
+        nc.gpsimd.memset(warm[:], 0.0)
+        pos = keep.tile([P, POS_BLOCKS], F32, name="pos")
+        nc.gpsimd.iota(pos[:], [[P, POS_BLOCKS]], base=0, channel_multiplier=1, allow_small_or_imprecise_dtypes=True)
+
+        xa, w0 = x_blocks[0], w_blocks[0]
+        for g0, g1 in ((0, 2), (2, PASSES)):
+            zero_planes(nc.vector, xa, g0, g1)
+            zero_planes(nc.vector, w0, g0, g1)
+        zero_planes(nc.gpsimd, x_blocks[1], 0, PASSES)
+        for cb in range(1, W_BLOCKS):
+            zero_planes(nc.gpsimd, w_blocks[cb], 0, PASSES)
+
+        w0_words, w0_scales, w0_col = w_source(0)
+        load_codes(xa, x_words, 0, 0, 2)
+        load_codes(w0, w0_words, w0_col, 0, 2)
+        load_scales(xa, x_scales, 0, 0, 2)
+        load_scales(w0, w0_scales, w0_col, 0, 2)
+        load_codes(xa, x_words, 0, 2, 4)
+        load_codes(w0, w0_words, w0_col, 2, 4)
+        load_scales(xa, x_scales, 0, 2, PASSES)
+        load_scales(w0, w0_scales, w0_col, 2, PASSES)
+        load_codes(xa, x_words, 0, 4, PASSES)
+        load_codes(w0, w0_words, w0_col, 4, PASSES)
+        load_codes(x_blocks[1], x_words, COLS, 0, PASSES)
+        load_scales(x_blocks[1], x_scales, COLS, 0, PASSES)
+        load_w(1)
+        load_w(2)
+
+        acc_warm = psum.tile([P, COLS], F32, name="acc_warm", tag="acc")
+        for i in range(10):
+            nc.tensor.matmul(acc_warm[:], warm[:, :P], warm[:], start=True, stop=True)
+
+        inv = keep.tile([P, HALF], F32, name="inv")
+        nc.vector.tensor_scalar(inv[:, 0:1], pos[:, 0:1], 0.0, 0.5 / math.pi, op0=ALU.mult, op1=ALU.add)
+        known = 1
+        while known < HALF:
+            nc.vector.tensor_scalar(
+                inv[:, known : 2 * known], inv[:, 0:known], BASE ** (-2.0 * known / HD), None, op0=ALU.mult
+            )
+            known *= 2
+        turns = keep.tile([P, POS_BLOCKS, HALF], F32, name="turns")
+        for pb in range(POS_BLOCKS):
+            nc.vector.tensor_scalar(turns[:, pb, :], inv[:], pos[:, pb : pb + 1], None, op0=ALU.mult)
+        whole = keep.tile([P, POS_BLOCKS, HALF], I32, name="whole")
+        nc.vector.tensor_copy(out=whole[:], in_=turns[:])
+        frac = keep.tile([P, POS_BLOCKS, HALF], F32, name="frac")
+        nc.vector.tensor_tensor(frac[:], turns[:], whole[:], ALU.subtract)
+        quarter = keep.tile([P, POS_BLOCKS, HALF], F32, name="quarter")
+        nc.vector.scalar_tensor_tensor(quarter[:], frac[:], -1.0, frac[:], op0=ALU.mult, op1=ALU.max)
+        quarter2 = keep.tile([P, POS_BLOCKS, HALF], F32, name="quarter2")
+        nc.vector.tensor_scalar(quarter2[:], quarter[:], -1.0, 0.25, op0=ALU.mult, op1=ALU.add)
+        cos_t = keep.tile([P, POS_BLOCKS, 2, HALF], F32, name="cos_t")
+        sin_t = keep.tile([P, POS_BLOCKS, 2, HALF], F32, name="sin_t")
+        two_pi = 2.0 * math.pi
+        nc.scalar.activation(sin_t[:, :, 0, :], frac[:], ACT.Sin, scale=-two_pi)
+        nc.scalar.activation(sin_t[:, :, 1, :], frac[:], ACT.Sin, scale=two_pi)
+        nc.scalar.activation(cos_t[:, :, 0, :], quarter2[:], ACT.Sin, scale=two_pi)
+        nc.scalar.activation(cos_t[:, :, 1, :], quarter2[:], ACT.Sin, scale=two_pi)
+
+        def multiply(acc, tt, cb, g, col0, n):
+            xc, xp = x_blocks[tt // 4]
+            wc, wp = w_blocks[cb]
+            m0 = (tt % 4) * P
+            nc.tensor.matmul_mx(
+                out=acc[:, 0:n],
+                lhsT=xc[:, g, 2 * m0 : 2 * (m0 + P)].bitcast(FP4X4),
+                lhsT_scale=xp[:, g, m0 : m0 + P],
+                rhs=wc[:, g, 2 * col0 : 2 * (col0 + n)].bitcast(FP4X4),
+                rhs_scale=wp[:, g, col0 : col0 + n],
+                start=(g == 0),
+                stop=(g == PASSES - 1),
+            )
+
+        def rotate(acc, tt, n):
+            h = n // HD
+            pb = tt % POS_BLOCKS
+            direct = rope.tile([P, HEADS, HD], F32, name="direct")
+            crossed = rope.tile([P, HEADS, 2, HALF], F32, name="crossed")
+            nc.vector.tensor_tensor(
+                direct[:, 0:h, :],
+                acc[:, 0:n].rearrange("p (h d) -> p h d", h=h),
+                cos_t[:, pb, :, :].rearrange("p t j -> p (t j)").unsqueeze(1).to_broadcast([P, h, HD]),
+                ALU.mult,
+            )
+            nc.vector.tensor_tensor(
+                crossed[:, 0:h, :, :],
+                acc[:, 0:n].rearrange("p (h t j) -> p h t j", h=h, t=2)[:, :, ::-1, :],
+                sin_t[:, pb, :, :].unsqueeze(1).to_broadcast([P, h, 2, HALF]),
+                ALU.mult,
+            )
+            return direct, crossed
+
+        def finish(item):
+            direct, crossed, tt, cb, col0, n = item
+            h = n // HD
+            nc.vector.tensor_tensor(
+                direct[:, 0:h, :],
+                direct[:, 0:h, :],
+                crossed[:, 0:h, :, :].rearrange("p h t j -> p h (t j)"),
+                ALU.add,
+            )
+            per = FEATURES // COLS
+            dst = out_q if cb < per else out_k
+            h0 = (cb % per) * HEADS + col0 // HD
+            s0 = (tt % POS_BLOCKS) * P
+            nc.scalar.dma_start(
+                out=dst[tt // POS_BLOCKS, h0 : h0 + h, s0 : s0 + P, :].rearrange("h s d -> s h d"),
+                in_=direct[:, 0:h, :],
+            )
+
+        pending = []
+
+        def epilogue(acc, tt, cb, col0, n):
+            direct, crossed = rotate(acc, tt, n)
+            if pending:
+                finish(pending.pop())
+            pending.append((direct, crossed, tt, cb, col0, n))
+
+        first = []
+        for tt in range(4):
+            first.append(psum.tile([P, COLS], F32, name="acc_first%d" % tt, tag="acc"))
+        for g in range(PASSES):
+            for tt in range(4):
+                multiply(first[tt], tt, 0, g, 0, COLS)
+        for tt in range(4):
+            epilogue(first[tt], tt, 0, 0, COLS)
+
+        for cb in range(W_BLOCKS):
+            for tt in range(4 if cb == 0 else 0, TOKEN_TILES):
+                last = cb == W_BLOCKS - 1 and tt == TOKEN_TILES - 1
+                for col0, n in ((0, 256), (256, 128), (384, 128)) if last else ((0, COLS),):
+                    acc = psum.tile([P, COLS], F32, name="acc")
+                    for g in range(PASSES):
+                        multiply(acc, tt, cb, g, col0, n)
+                    epilogue(acc, tt, cb, col0, n)
+            if cb + 3 < W_BLOCKS:
+                load_w(cb + 3)
+        finish(pending.pop())

@@ -79,7 +79,7 @@ def tile_multiheadattention_pa_kernel(
         nc.gpsimd.iota(pos[:], [[P, POS_BLOCKS]], base=0, channel_multiplier=1, allow_small_or_imprecise_dtypes=True)
 
         xa, w0 = x_blocks[0], w_blocks[0]
-        for g0, g1 in ((0, 2), (2, PASSES)):
+        for g0, g1 in ((0, 4), (4, PASSES)):
             zero_planes(nc.vector, xa, g0, g1)
             zero_planes(nc.vector, w0, g0, g1)
         zero_planes(nc.gpsimd, x_blocks[1], 0, PASSES)
@@ -87,14 +87,14 @@ def tile_multiheadattention_pa_kernel(
             zero_planes(nc.gpsimd, w_blocks[cb], 0, PASSES)
 
         w0_words, w0_scales, w0_col = w_source(0)
-        load_codes(xa, x_words, 0, 0, 2)
-        load_codes(w0, w0_words, w0_col, 0, 2)
-        load_scales(xa, x_scales, 0, 0, 2)
-        load_scales(w0, w0_scales, w0_col, 0, 2)
-        load_codes(xa, x_words, 0, 2, 4)
-        load_codes(w0, w0_words, w0_col, 2, 4)
-        load_scales(xa, x_scales, 0, 2, PASSES)
-        load_scales(w0, w0_scales, w0_col, 2, PASSES)
+        load_codes(xa, x_words, 0, 0, 1)
+        load_codes(w0, w0_words, w0_col, 0, 1)
+        load_scales(xa, x_scales, 0, 0, 4)
+        load_scales(w0, w0_scales, w0_col, 0, 4)
+        load_codes(xa, x_words, 0, 1, 4)
+        load_codes(w0, w0_words, w0_col, 1, 4)
+        load_scales(xa, x_scales, 0, 4, PASSES)
+        load_scales(w0, w0_scales, w0_col, 4, PASSES)
         load_codes(xa, x_words, 0, 4, PASSES)
         load_codes(w0, w0_words, w0_col, 4, PASSES)
         load_codes(x_blocks[1], x_words, COLS, 0, PASSES)
@@ -103,7 +103,7 @@ def tile_multiheadattention_pa_kernel(
         load_w(2)
 
         acc_warm = psum.tile([P, COLS], F32, name="acc_warm", tag="acc")
-        for i in range(10):
+        for i in range(12):
             nc.tensor.matmul(acc_warm[:], warm[:, :P], warm[:], start=True, stop=True)
 
         inv = keep.tile([P, HALF], F32, name="inv")
@@ -125,13 +125,12 @@ def tile_multiheadattention_pa_kernel(
         nc.vector.scalar_tensor_tensor(quarter[:], frac[:], -1.0, frac[:], op0=ALU.mult, op1=ALU.max)
         quarter2 = keep.tile([P, POS_BLOCKS, HALF], F32, name="quarter2")
         nc.vector.tensor_scalar(quarter2[:], quarter[:], -1.0, 0.25, op0=ALU.mult, op1=ALU.add)
-        cos_t = keep.tile([P, POS_BLOCKS, 2, HALF], F32, name="cos_t")
-        sin_t = keep.tile([P, POS_BLOCKS, 2, HALF], F32, name="sin_t")
+        factors = keep.tile([P, POS_BLOCKS, 2, 2, HALF], F32, name="factors")
         two_pi = 2.0 * math.pi
-        nc.scalar.activation(sin_t[:, :, 0, :], frac[:], ACT.Sin, scale=-two_pi)
-        nc.scalar.activation(sin_t[:, :, 1, :], frac[:], ACT.Sin, scale=two_pi)
-        nc.scalar.activation(cos_t[:, :, 0, :], quarter2[:], ACT.Sin, scale=two_pi)
-        nc.scalar.activation(cos_t[:, :, 1, :], quarter2[:], ACT.Sin, scale=two_pi)
+        nc.scalar.activation(factors[:, :, 0, 0, :], quarter2[:], ACT.Sin, scale=two_pi)
+        nc.scalar.activation(factors[:, :, 0, 1, :], quarter2[:], ACT.Sin, scale=two_pi)
+        nc.scalar.activation(factors[:, :, 1, 0, :], frac[:], ACT.Sin, scale=two_pi)
+        nc.scalar.activation(factors[:, :, 1, 1, :], frac[:], ACT.Sin, scale=-two_pi)
 
         def multiply(acc, tt, cb, g, col0, n):
             xc, xp = x_blocks[tt // 4]
@@ -150,47 +149,42 @@ def tile_multiheadattention_pa_kernel(
         def rotate(acc, tt, n):
             h = n // HD
             pb = tt % POS_BLOCKS
-            direct = rope.tile([P, HEADS, HD], F32, name="direct")
-            crossed = rope.tile([P, HEADS, 2, HALF], F32, name="crossed")
+            prod = rope.tile([P, 2, HEADS, HD], F32, name="prod")
             nc.vector.tensor_tensor(
-                direct[:, 0:h, :],
-                acc[:, 0:n].rearrange("p (h d) -> p h d", h=h),
-                cos_t[:, pb, :, :].rearrange("p t j -> p (t j)").unsqueeze(1).to_broadcast([P, h, HD]),
+                prod[:, :, 0:h, :],
+                acc[:, 0:n].rearrange("p (h d) -> p h d", h=h).unsqueeze(1).to_broadcast([P, 2, h, HD]),
+                factors[:, pb].rearrange("p v t j -> p v (t j)").unsqueeze(2).to_broadcast([P, 2, h, HD]),
                 ALU.mult,
             )
-            nc.vector.tensor_tensor(
-                crossed[:, 0:h, :, :],
-                acc[:, 0:n].rearrange("p (h t j) -> p h t j", h=h, t=2)[:, :, ::-1, :],
-                sin_t[:, pb, :, :].unsqueeze(1).to_broadcast([P, h, 2, HALF]),
-                ALU.mult,
-            )
-            return direct, crossed
+            return prod
 
-        def finish(item):
-            direct, crossed, tt, cb, col0, n = item
+        def finish(engine, item):
+            prod, tt, cb, col0, n = item
             h = n // HD
-            nc.vector.tensor_tensor(
-                direct[:, 0:h, :],
-                direct[:, 0:h, :],
-                crossed[:, 0:h, :, :].rearrange("p h t j -> p h (t j)"),
-                ALU.add,
-            )
+            by_half = prod[:, :, 0:h, :].rearrange("p v h (t j) -> p v h t j", t=2)
+            engine.tensor_tensor(by_half[:, 0], by_half[:, 0], by_half[:, 1, :, ::-1, :], ALU.add)
             per = FEATURES // COLS
             dst = out_q if cb < per else out_k
             h0 = (cb % per) * HEADS + col0 // HD
             s0 = (tt % POS_BLOCKS) * P
             nc.scalar.dma_start(
                 out=dst[tt // POS_BLOCKS, h0 : h0 + h, s0 : s0 + P, :].rearrange("h s d -> s h d"),
-                in_=direct[:, 0:h, :],
+                in_=prod[:, 0, 0:h, :],
             )
 
         pending = []
 
         def epilogue(acc, tt, cb, col0, n):
-            direct, crossed = rotate(acc, tt, n)
+            item = (rotate(acc, tt, n), tt, cb, col0, n)
             if pending:
-                finish(pending.pop())
-            pending.append((direct, crossed, tt, cb, col0, n))
+                finish(nc.vector, pending.pop())
+            closing = cb == W_BLOCKS - 1
+            if closing and (tt in (TOKEN_TILES - 3, TOKEN_TILES - 2) or col0 == 256):
+                finish(nc.gpsimd, item)
+            elif closing and col0 == 384:
+                finish(nc.vector, item)
+            else:
+                pending.append(item)
 
         first = []
         for tt in range(4):
@@ -211,4 +205,3 @@ def tile_multiheadattention_pa_kernel(
                     epilogue(acc, tt, cb, col0, n)
             if cb + 3 < W_BLOCKS:
                 load_w(cb + 3)
-        finish(pending.pop())

import math
from contextlib import ExitStack

import concourse.mybir as mybir

F32 = mybir.dt.float32
BF16 = mybir.dt.bfloat16
I32 = mybir.dt.int32
U8 = mybir.dt.uint8
FP4X4 = mybir.dt.float4_e2m1fn_x4
ACT = mybir.ActivationFunctionType
ALU = mybir.AluOpType

B, S, H, NH, HD = 2, 512, 4096, 16, 128
P = 128
TOKENS = B * S
FEATURES = NH * HD
PASSES = H // 512
COLS = 512
HEADS = COLS // HD
HALF = HD // 2
POS_BLOCKS = S // P
TOKEN_TILES = TOKENS // P
W_BLOCKS = 2 * FEATURES // COLS
BASE = 10000.0

FLOPS = 2 * TOKENS * H * 2 * FEATURES


def tile_multiheadattention_pa_kernel(
    tc, x_words, x_scales, wq_words, wq_scales, wk_words, wk_scales, out_q, out_k
):
    nc = tc.nc
    with ExitStack() as ctx:
        ctx.enter_context(tc.manual_schedule())
        keep = ctx.enter_context(tc.tile_pool(name="keep", bufs=1))
        rope = ctx.enter_context(tc.tile_pool(name="rope", bufs=6))
        psum = ctx.enter_context(tc.psum_pool(name="psum", bufs=8))

        def new_block(label):
            codes = keep.tile([P, PASSES, 2 * COLS], U8, name="codes_" + label, align_bytes=256)
            planes = keep.tile([P, PASSES, COLS], U8, name="planes_" + label, align_bytes=256)
            return codes, planes

        def zero_planes(engine, block, g0, g1):
            engine.memset(block[1][:, g0:g1, :].rearrange("p g n -> p (g n)").bitcast(I32), 0)

        def load_codes(block, words, col0, g0, g1):
            nc.sync.dma_start(
                out=block[0][:, g0:g1, :],
                in_=words[g0:g1, :, 2 * col0 : 2 * (col0 + COLS)].rearrange("g p b -> p g b"),
            )

        def load_scales(block, scales, col0, g0, g1):
            for q in range(4):
                nc.sync.dma_start(
                    out=block[1][32 * q : 32 * q + 4, g0:g1, :].bitcast(I32),
                    in_=scales[g0:g1, 4 * q : 4 * q + 4, col0 : col0 + COLS]
                    .rearrange("g r n -> r g n")
                    .bitcast(I32),
                )

        x_blocks = [new_block("x%d" % i) for i in range(TOKENS // COLS)]
        w_blocks = [new_block("w%d" % i) for i in range(W_BLOCKS)]

        def w_source(cb):
            per = FEATURES // COLS
            words, scales = (wq_words, wq_scales) if cb < per else (wk_words, wk_scales)
            return words, scales, (cb % per) * COLS

        def load_w(cb):
            words, scales, col0 = w_source(cb)
            load_codes(w_blocks[cb], words, col0, 0, PASSES)
            load_scales(w_blocks[cb], scales, col0, 0, PASSES)

        warm = keep.tile([P, COLS], BF16, name="warm")
        nc.gpsimd.memset(warm[:], 0.0)
        pos = keep.tile([P, POS_BLOCKS], F32, name="pos")
        nc.gpsimd.iota(pos[:], [[P, POS_BLOCKS]], base=0, channel_multiplier=1, allow_small_or_imprecise_dtypes=True)

        xa, w0 = x_blocks[0], w_blocks[0]
        for g0, g1 in ((0, 4), (4, PASSES)):
            zero_planes(nc.vector, xa, g0, g1)
            zero_planes(nc.vector, w0, g0, g1)
        zero_planes(nc.gpsimd, x_blocks[1], 0, PASSES)
        for cb in range(1, W_BLOCKS):
            zero_planes(nc.gpsimd, w_blocks[cb], 0, PASSES)

        w0_words, w0_scales, w0_col = w_source(0)
        load_codes(xa, x_words, 0, 0, 1)
        load_codes(w0, w0_words, w0_col, 0, 1)
        load_scales(xa, x_scales, 0, 0, 4)
        load_scales(w0, w0_scales, w0_col, 0, 4)
        load_codes(xa, x_words, 0, 1, 4)
        load_codes(w0, w0_words, w0_col, 1, 4)
        load_scales(xa, x_scales, 0, 4, PASSES)
        load_scales(w0, w0_scales, w0_col, 4, PASSES)
        load_codes(xa, x_words, 0, 4, PASSES)
        load_codes(w0, w0_words, w0_col, 4, PASSES)
        load_codes(x_blocks[1], x_words, COLS, 0, PASSES)
        load_scales(x_blocks[1], x_scales, COLS, 0, PASSES)
        load_w(1)
        load_w(2)

        acc_warm = psum.tile([P, COLS], F32, name="acc_warm", tag="acc")
        for i in range(12):
            nc.tensor.matmul(acc_warm[:], warm[:, :P], warm[:], start=True, stop=True)

        inv = keep.tile([P, HALF], F32, name="inv")
        nc.vector.tensor_scalar(inv[:, 0:1], pos[:, 0:1], 0.0, 0.5 / math.pi, op0=ALU.mult, op1=ALU.add)
        known = 1
        while known < HALF:
            nc.vector.tensor_scalar(
                inv[:, known : 2 * known], inv[:, 0:known], BASE ** (-2.0 * known / HD), None, op0=ALU.mult
            )
            known *= 2
        turns = keep.tile([P, POS_BLOCKS, HALF], F32, name="turns")
        for pb in range(POS_BLOCKS):
            nc.vector.tensor_scalar(turns[:, pb, :], inv[:], pos[:, pb : pb + 1], None, op0=ALU.mult)
        whole = keep.tile([P, POS_BLOCKS, HALF], I32, name="whole")
        nc.vector.tensor_copy(out=whole[:], in_=turns[:])
        frac = keep.tile([P, POS_BLOCKS, HALF], F32, name="frac")
        nc.vector.tensor_tensor(frac[:], turns[:], whole[:], ALU.subtract)
        quarter = keep.tile([P, POS_BLOCKS, HALF], F32, name="quarter")
        nc.vector.scalar_tensor_tensor(quarter[:], frac[:], -1.0, frac[:], op0=ALU.mult, op1=ALU.max)
        quarter2 = keep.tile([P, POS_BLOCKS, HALF], F32, name="quarter2")
        nc.vector.tensor_scalar(quarter2[:], quarter[:], -1.0, 0.25, op0=ALU.mult, op1=ALU.add)
        factors = keep.tile([P, POS_BLOCKS, 2, 2, HALF], F32, name="factors")
        two_pi = 2.0 * math.pi
        nc.scalar.activation(factors[:, :, 0, 0, :], quarter2[:], ACT.Sin, scale=two_pi)
        nc.scalar.activation(factors[:, :, 0, 1, :], quarter2[:], ACT.Sin, scale=two_pi)
        nc.scalar.activation(factors[:, :, 1, 0, :], frac[:], ACT.Sin, scale=two_pi)
        nc.scalar.activation(factors[:, :, 1, 1, :], frac[:], ACT.Sin, scale=-two_pi)

        def multiply(acc, tt, cb, g, col0, n):
            xc, xp = x_blocks[tt // 4]
            wc, wp = w_blocks[cb]
            m0 = (tt % 4) * P
            nc.tensor.matmul_mx(
                out=acc[:, 0:n],
                lhsT=xc[:, g, 2 * m0 : 2 * (m0 + P)].bitcast(FP4X4),
                lhsT_scale=xp[:, g, m0 : m0 + P],
                rhs=wc[:, g, 2 * col0 : 2 * (col0 + n)].bitcast(FP4X4),
                rhs_scale=wp[:, g, col0 : col0 + n],
                start=(g == 0),
                stop=(g == PASSES - 1),
            )

        def rotate(acc, tt, n):
            h = n // HD
            pb = tt % POS_BLOCKS
            prod = rope.tile([P, 2, HEADS, HD], F32, name="prod")
            nc.vector.tensor_tensor(
                prod[:, :, 0:h, :],
                acc[:, 0:n].rearrange("p (h d) -> p h d", h=h).unsqueeze(1).to_broadcast([P, 2, h, HD]),
                factors[:, pb].rearrange("p v t j -> p v (t j)").unsqueeze(2).to_broadcast([P, 2, h, HD]),
                ALU.mult,
            )
            return prod

        def finish(engine, item):
            prod, tt, cb, col0, n = item
            h = n // HD
            by_half = prod[:, :, 0:h, :].rearrange("p v h (t j) -> p v h t j", t=2)
            engine.tensor_tensor(by_half[:, 0], by_half[:, 0], by_half[:, 1, :, ::-1, :], ALU.add)
            per = FEATURES // COLS
            dst = out_q if cb < per else out_k
            h0 = (cb % per) * HEADS + col0 // HD
            s0 = (tt % POS_BLOCKS) * P
            nc.scalar.dma_start(
                out=dst[tt // POS_BLOCKS, h0 : h0 + h, s0 : s0 + P, :].rearrange("h s d -> s h d"),
                in_=prod[:, 0, 0:h, :],
            )

        pending = []

        def epilogue(acc, tt, cb, col0, n):
            item = (rotate(acc, tt, n), tt, cb, col0, n)
            if pending:
                finish(nc.vector, pending.pop())
            closing = cb == W_BLOCKS - 1
            if closing and (tt in (TOKEN_TILES - 3, TOKEN_TILES - 2) or col0 == 256):
                finish(nc.gpsimd, item)
            elif closing and col0 == 384:
                finish(nc.vector, item)
            else:
                pending.append(item)

        first = []
        for tt in range(4):
            first.append(psum.tile([P, COLS], F32, name="acc_first%d" % tt, tag="acc"))
        for g in range(PASSES):
            for tt in range(4):
                multiply(first[tt], tt, 0, g, 0, COLS)
        for tt in range(4):
            epilogue(first[tt], tt, 0, 0, COLS)

        for cb in range(W_BLOCKS):
            for tt in range(4 if cb == 0 else 0, TOKEN_TILES):
                last = cb == W_BLOCKS - 1 and tt == TOKEN_TILES - 1
                for col0, n in ((0, 256), (256, 128), (384, 128)) if last else ((0, COLS),):
                    acc = psum.tile([P, COLS], F32, name="acc")
                    for g in range(PASSES):
                        multiply(acc, tt, cb, g, col0, n)
                    epilogue(acc, tt, cb, col0, n)
            if cb + 3 < W_BLOCKS:
                load_w(cb + 3)
